import numpy as np
import ml_dtypes


def mxq(x, axis, fmt="e4m3"):
    dtype, down = {"e4m3": (ml_dtypes.float8_e4m3fn, 7), "e5m2": (ml_dtypes.float8_e5m2, 14)}[fmt]
    v = np.moveaxis(np.asarray(x, np.float32).astype(ml_dtypes.bfloat16).astype(np.float64), axis, -1)
    blocks = v.reshape(v.shape[:-1] + (-1, 32))
    amax = np.abs(blocks).max(-1, keepdims=True)
    byte = np.maximum(np.where(amax > 0, np.frexp(amax)[1] - 1 + 127, 0) - down, 1)
    scale = np.exp2(byte - 127.0)
    codes = (blocks / scale).astype(np.float32).astype(dtype).astype(np.float64)
    return np.moveaxis((codes * scale).reshape(v.shape), -1, axis)


WIDE = False


def mx_kscale(k):
    if not WIDE:
        return np.ones(k)
    levels = np.array([10, -10, 5, -5, 0])
    if k % 512:
        return np.exp2(np.random.permutation(np.resize(levels, k // 32))).repeat(32)
    a = np.empty((k // 512, 16))
    for p in range(k // 512):
        a[p, :8] = np.random.permutation(np.resize(levels, 8))
        for g in range(8):
            far = levels[np.abs(levels - a[p, g]) >= 10]
            a[p, g + 8] = far[np.random.randint(len(far))]
    return np.exp2(a.ravel()).repeat(32)


BF16 = ml_dtypes.bfloat16


def bf(x):
    return np.asarray(x, np.float32).astype(BF16)


def f64(x):
    return np.asarray(x).astype(np.float64)


B, S, D, F1, F2, F3, F4 = 128, 4, 256, 1024, 2048, 1024, 512
K = D + D


def setup_inputs():
    s, t = mx_kscale(K), mx_kscale(F1)
    return {"x1": bf(np.random.standard_normal((B, S, D)) * s[:D]),
            "x2": bf(np.random.standard_normal((B, S, D)) * s[D:]),
            "W1": bf(np.random.standard_normal((S, K, F1)) * 1.0 / np.sqrt(K) / s[None, :, None] * t[None, None, :]),
            "b1": bf(np.random.standard_normal((S, F1)) * 0.3 * t),
            "W2": bf(np.random.standard_normal((S, F1, F2)) * 1.4 / np.sqrt(F1) / t[None, :, None]),
            "b2": bf(np.random.standard_normal((S, F2)) * 0.3)}


def reference(x1, x2, W1, b1, W2, b2):
    x = np.concatenate([f64(x1), f64(x2)], axis=-1).transpose(1, 0, 2)
    h = np.maximum((mxq(x, 2, "e4m3") @ mxq(f64(W1), 1, "e4m3")) + f64(b1)[:, None, :], 0.0)
    y = (mxq(h, 2, "e4m3") @ mxq(f64(W2), 1, "e4m3")) + f64(b2)[:, None, :]
    return y.transpose(1, 0, 2)

@@ -1,0 +1,268 @@
+from contextlib import ExitStack
+
+import concourse.mybir as mybir
+from concourse.masks import make_identity
+
+BF16 = mybir.dt.bfloat16
+F32 = mybir.dt.float32
+U32 = mybir.dt.uint32
+U8 = mybir.dt.uint8
+FP8X4 = mybir.dt.float8_e4m3fn_x4
+ADD = mybir.AluOpType.add
+
+P = 128
+PACK = 4
+K_PASS = P * PACK
+
+B, S, D, F1, F2 = 128, 4, 256, 1024, 2048
+STREAMS = 2
+PAIR = 2
+PASSES2 = F1 // K_PASS
+N_PASS = 512
+SLAB_COLS = 1024
+PASSES_PER_SLAB = SLAB_COLS // N_PASS
+HALVES = F2 // SLAB_COLS
+SLABS_PER_W2 = PASSES2 * HALVES
+SLABS = S + S * SLABS_PER_W2
+RESIDENT = 14
+RUN = 4
+
+VECTOR_COLS = 416
+
+FLOPS = 2 * B * S * (STREAMS * D * F1 + F1 * F2)
+
+
+def tile_simplefusionmodule_pa_kernel(tc, x1, x2, W1, b1, W2, b2, out):
+    nc = tc.nc
+    with ExitStack() as ctx:
+        ctx.enter_context(tc.manual_schedule())
+        const = ctx.enter_context(tc.tile_pool(name="const", bufs=1))
+        raw_pool = ctx.enter_context(tc.tile_pool(name="raw_pool", bufs=RESIDENT))
+        grouped_pool = ctx.enter_context(tc.tile_pool(name="grouped_pool", bufs=4))
+        codes_pool = ctx.enter_context(tc.tile_pool(name="codes_pool", bufs=4))
+        style_pool = ctx.enter_context(tc.tile_pool(name="style_pool", bufs=2))
+        h_pool = ctx.enter_context(tc.tile_pool(name="h_pool", bufs=S))
+        out_pool = ctx.enter_context(tc.tile_pool(name="out_pool", bufs=S * F2 // N_PASS))
+        prep_psum = ctx.enter_context(tc.psum_pool(name="prep_psum", bufs=2))
+        h_psum = ctx.enter_context(tc.psum_pool(name="h_psum", bufs=PASSES2))
+        acc_psum = ctx.enter_context(tc.psum_pool(name="acc_psum", bufs=F2 // N_PASS))
+
+        raw_of = {}
+        grouped_of = {}
+        codes_of = {}
+        h_acc_of = {}
+        h_codes_of = {}
+        acc_of = {}
+        spread_of = {}
+        b2_of = {}
+
+        def w2_place(j):
+            s, quarter = divmod(j - S, SLABS_PER_W2)
+            g, w = divmod(quarter, HALVES)
+            return s, g, w
+
+        def load(j):
+            raw = raw_pool.tile([P, PACK, SLAB_COLS], BF16)
+            if j < S:
+                part = W1[j]
+            else:
+                s, g, w = w2_place(j)
+                part = W2[s, g * K_PASS : (g + 1) * K_PASS, w * SLAB_COLS : (w + 1) * SLAB_COLS]
+            nc.sync.dma_start(out=raw[:], in_=part.rearrange("(p t) n -> p t n", t=PACK))
+            raw_of[j] = raw
+
+        def regroup(j):
+            grouped = grouped_pool.tile([P, SLAB_COLS, PACK], BF16, align_bytes=64)
+            if j < S:
+                dst = grouped[:].rearrange("p (g r m) t -> p g m t r", g=PASSES2, r=PACK)
+                src = raw_of[j][:].rearrange("p t (g m r) -> p g m t r", g=PASSES2, r=PACK)
+                cut = VECTOR_COLS // PASSES2 // PACK
+                nc.vector.tensor_copy(out=dst[:, :, :cut], in_=src[:, :, :cut])
+                nc.scalar.copy(out=dst[:, :, cut:], in_=src[:, :, cut:])
+            else:
+                dst = grouped[:].rearrange("p (c i) t -> p c t i", i=RUN)
+                src = raw_of[j][:].rearrange("p t (c i) -> p c t i", i=RUN)
+                cut = VECTOR_COLS // RUN
+                nc.vector.tensor_copy(out=dst[:, :cut], in_=src[:, :cut])
+                nc.scalar.copy(out=dst[:, cut:], in_=src[:, cut:])
+            grouped_of[j] = grouped
+
+        def quantise(j):
+            codes = codes_pool.tile([P, SLAB_COLS], U32, align_bytes=64)
+            scales = codes_pool.tile([P, SLAB_COLS], U8, align_bytes=64)
+            nc.vector.quantize_mx(
+                out=codes[:].bitcast(FP8X4),
+                scales=scales[:],
+                in_=grouped_of[j][:].rearrange("p c t -> p (c t)"),
+            )
+            codes_of[j] = (codes, scales)
+
+        def multiply(j):
+            codes, scales = codes_of[j]
+            if j < S:
+                h_acc_of[j] = []
+                for g in range(PASSES2):
+                    h_acc = h_psum.tile([P, PACK, B], F32)
+                    for t in range(PACK):
+                        feats = slice((g * PACK + t) * P, (g * PACK + t + 1) * P)
+                        nc.tensor.matmul_mx(
+                            out=h_acc[:, t, :],
+                            lhsT=codes[:, feats].bitcast(FP8X4),
+                            lhsT_scale=scales[:, feats],
+                            rhs=x_codes[:, j * B : (j + 1) * B].bitcast(FP8X4),
+                            rhs_scale=x_scales[:, j * B : (j + 1) * B],
+                            start=True,
+                            stop=True,
+                        )
+                    h_acc_of[j].append(h_acc)
+            else:
+                s, g, w = w2_place(j)
+                h_codes, h_scales = h_codes_of[s]
+                for i in range(PASSES_PER_SLAB):
+                    n = w * PASSES_PER_SLAB + i
+                    if g == 0:
+                        bank = acc_psum.tile([P, N_PASS], F32)
+                        acc_of[(s, n)] = bank
+                    nc.tensor.matmul_mx(
+                        out=acc_of[(s, n)][:],
+                        lhsT=h_codes[:, g * B : (g + 1) * B].bitcast(FP8X4),
+                        lhsT_scale=h_scales[:, g * B : (g + 1) * B],
+                        rhs=codes[:, i * N_PASS : (i + 1) * N_PASS].bitcast(FP8X4),
+                        rhs_scale=scales[:, i * N_PASS : (i + 1) * N_PASS],
+                        start=(g == 0),
+                        stop=(g == PASSES2 - 1),
+                    )
+
+        def drain_h(s):
+            h_grouped = style_pool.tile([P, PASSES2, B, PACK], BF16, align_bytes=64)
+            h_codes = h_pool.tile([P, PASSES2 * B], U32, align_bytes=64)
+            h_scales = h_pool.tile([P, PASSES2 * B], U8, align_bytes=64)
+            for g in range(PASSES2):
+                b1_row = s * PASSES2 + g
+                nc.vector.tensor_tensor(
+                    out=h_grouped[:, g],
+                    in0=h_acc_of[s][g][:].rearrange("p t b -> p b t"),
+                    in1=b1_cols[:, b1_row].unsqueeze(1).to_broadcast([P, B, PACK]),
+                    op=ADD,
+                )
+            for g in range(PASSES2):
+                nc.vector.tensor_scalar_max(h_grouped[:, g], h_grouped[:, g], 0.0)
+            for g in range(PASSES2):
+                nc.vector.quantize_mx(
+                    out=h_codes[:, g * B : (g + 1) * B].bitcast(FP8X4),
+                    scales=h_scales[:, g * B : (g + 1) * B],
+                    in_=h_grouped[:, g].rearrange("p b t -> p (b t)"),
+                )
+            h_codes_of[s] = (h_codes, h_scales)
+
+        def drain_out(s, w):
+            for i in range(PASSES_PER_SLAB):
+                n = w * PASSES_PER_SLAB + i
+                cols = slice(n * N_PASS, (n + 1) * N_PASS)
+                result = out_pool.tile([P, N_PASS], F32)
+                nc.vector.tensor_tensor(
+                    out=result[:], in0=acc_of[(s, n)][:], in1=b2_of[s][:, cols], op=ADD
+                )
+                nc.sync.dma_start(out=out[:, s, cols], in_=result[:])
+
+        def drain(j):
+            if j < S:
+                drain_h(j)
+            else:
+                s, g, w = w2_place(j)
+                if g == PASSES2 - 1:
+                    drain_out(s, w)
+
+        def spread_b2(s):
+            spread_of[s] = []
+            for w in range(HALVES):
+                spread = prep_psum.tile([P, SLAB_COLS], BF16, tag="prep")
+                for c in range(SLAB_COLS // P):
+                    col = (s * F2 + w * SLAB_COLS) // P + c
+                    nc.tensor.transpose(
+                        spread[:, c * P : (c + 1) * P],
+                        b2_cols[:, col : col + 1].to_broadcast([P, P]),
+                        ident_bf[:],
+                    )
+                spread_of[s].append(spread)
+
+        def copy_b2(s):
+            b2_all = style_pool.tile([P, F2], BF16)
+            for w in range(HALVES):
+                nc.scalar.copy(
+                    out=b2_all[:, w * SLAB_COLS : (w + 1) * SLAB_COLS], in_=spread_of[s][w][:]
+                )
+            b2_of[s] = b2_all
+
+        B1_ROWS = S * PASSES2
+        B2_ROWS = S * F2 // P
+        b1_rows = const.tile([P, K_PASS], BF16)
+        nc.vector.memset(b1_rows[:], 0.0)
+        nc.sync.dma_start(
+            out=b1_rows[0:B1_ROWS, :], in_=b1.rearrange("s (g k) -> (s g) k", k=K_PASS)
+        )
+        b2_rows = const.tile([P, P], BF16)
+        nc.vector.memset(b2_rows[B2_ROWS:P, :], 0.0)
+        nc.sync.dma_start(
+            out=b2_rows[0:B2_ROWS, :], in_=b2.rearrange("s (c p) -> (s c) p", p=P)
+        )
+        x_both = const.tile([P, S, STREAMS * D], BF16)
+        nc.sync.dma_start(out=x_both[:, :, 0:D], in_=x1)
+        nc.sync.dma_start(out=x_both[:, :, D : STREAMS * D], in_=x2)
+        for j in range(RESIDENT):
+            load(j)
+
+        ident_bf = const.tile([P, P], BF16)
+        make_identity(nc, ident_bf[:])
+        ident_f32 = const.tile([P, P], F32)
+        make_identity(nc, ident_f32[:])
+
+        bias_cols = prep_psum.tile([P, PACK + 1, P], BF16, tag="prep")
+        for t in range(PACK):
+            nc.tensor.transpose(bias_cols[:, t], b1_rows[:, t:K_PASS:PACK], ident_bf[:])
+        nc.tensor.transpose(bias_cols[:, PACK], b2_rows[:], ident_bf[:])
+        b1_cols = const.tile([P, B1_ROWS, PACK], F32)
+        nc.vector.tensor_copy(
+            out=b1_cols[:], in_=bias_cols[:, 0:PACK, 0:B1_ROWS].rearrange("p t r -> p r t")
+        )
+        b2_cols = const.tile([P, B2_ROWS], BF16)
+        nc.vector.tensor_copy(out=b2_cols[:], in_=bias_cols[:, PACK, 0:B2_ROWS])
+
+        x_words = x_both[:].bitcast(F32)
+        x_grouped = const.tile([P, S, B, PAIR], F32, align_bytes=64)
+        STYLES_PER_BANK = 2
+        for s0 in range(0, S, STYLES_PER_BANK):
+            x_t = prep_psum.tile([P, STYLES_PER_BANK, PAIR, B], F32, tag="prep")
+            for i in range(STYLES_PER_BANK):
+                for u in range(PAIR):
+                    nc.tensor.transpose(x_t[:, i, u, :], x_words[:, s0 + i, u::PAIR], ident_f32[:])
+            nc.vector.tensor_copy(
+                out=x_grouped[:, s0 : s0 + STYLES_PER_BANK],
+                in_=x_t[:].rearrange("p s u b -> p s b u"),
+            )
+        x_codes = const.tile([P, S * B], U32, align_bytes=64)
+        x_scales = const.tile([P, S * B], U8, align_bytes=64)
+        nc.vector.quantize_mx(
+            out=x_codes[:].bitcast(FP8X4),
+            scales=x_scales[:],
+            in_=x_grouped[:].bitcast(BF16).rearrange("p s b t -> p (s b t)"),
+        )
+        spread_b2(0)
+
+        for step in range(SLABS + 3):
+            if step < SLABS:
+                regroup(step)
+                if step + RESIDENT < SLABS:
+                    load(step + RESIDENT)
+                if step >= S:
+                    s, g, w = w2_place(step)
+                    if (g, w) == (0, 0):
+                        copy_b2(s)
+                    if (g, w) == (0, 1) and s + 1 < S:
+                        spread_b2(s + 1)
+            if 0 <= step - 1 < SLABS:
+                quantise(step - 1)
+            if 0 <= step - 3:
+                drain(step - 3)
+            if 0 <= step - 2 < SLABS:
+                multiply(step - 2)

@@ -27,7 +27,7 @@ SLABS = S + S * SLABS_PER_W2
 RESIDENT = 14
 RUN = 4
 
-VECTOR_COLS = 416
+VECTOR_SHARE = 400
 
 FLOPS = 2 * B * S * (STREAMS * D * F1 + F1 * F2)
 
@@ -42,86 +42,102 @@ def tile_simplefusionmodule_pa_kernel(tc, x1, x2, W1, b1, W2, b2, out):
         codes_pool = ctx.enter_context(tc.tile_pool(name="codes_pool", bufs=4))
         style_pool = ctx.enter_context(tc.tile_pool(name="style_pool", bufs=2))
         h_pool = ctx.enter_context(tc.tile_pool(name="h_pool", bufs=S))
-        out_pool = ctx.enter_context(tc.tile_pool(name="out_pool", bufs=S * F2 // N_PASS))
+        out_pool = ctx.enter_context(tc.tile_pool(name="out_pool", bufs=10))
         prep_psum = ctx.enter_context(tc.psum_pool(name="prep_psum", bufs=2))
         h_psum = ctx.enter_context(tc.psum_pool(name="h_psum", bufs=PASSES2))
         acc_psum = ctx.enter_context(tc.psum_pool(name="acc_psum", bufs=F2 // N_PASS))
+
+        W1_SLABS = [("W1", 0, 0), ("W1", 0, 1)] + [("W1", s, None) for s in range(1, S)]
+        W2_SLABS = [("W2", s, (g, w)) for s in range(S) for w in range(HALVES) for g in range(PASSES2)]
+        slabs = W1_SLABS + W2_SLABS
+        units = [(j, 0, SLAB_COLS) for j in range(len(slabs))]
+        units[0] = (0, 0, K_PASS)
+        units[1] = (1, 0, K_PASS)
+        j_last = len(slabs) - 1
+        units[-2:] = [(j, c, N_PASS) for c in (0, N_PASS) for j in (j_last - 1, j_last)]
 
         raw_of = {}
         grouped_of = {}
         codes_of = {}
         h_acc_of = {}
+        h_grouped_of = {}
         h_codes_of = {}
         acc_of = {}
         spread_of = {}
         b2_of = {}
 
-        def w2_place(j):
-            s, quarter = divmod(j - S, SLABS_PER_W2)
-            g, w = divmod(quarter, HALVES)
-            return s, g, w
-
         def load(j):
-            raw = raw_pool.tile([P, PACK, SLAB_COLS], BF16)
-            if j < S:
-                part = W1[j]
+            matrix, s, where = slabs[j]
+            if matrix == "W1" and where is None:
+                raw = raw_pool.tile([P, PACK, SLAB_COLS], BF16, tag="raw")
+                part = W1[s]
+            elif matrix == "W1":
+                raw = const.tile([P, PACK, K_PASS], BF16, tag="first%d" % where)
+                part = W1[s, :, where * K_PASS : (where + 1) * K_PASS]
             else:
-                s, g, w = w2_place(j)
+                g, w = where
+                raw = raw_pool.tile([P, PACK, SLAB_COLS], BF16, tag="raw")
                 part = W2[s, g * K_PASS : (g + 1) * K_PASS, w * SLAB_COLS : (w + 1) * SLAB_COLS]
             nc.sync.dma_start(out=raw[:], in_=part.rearrange("(p t) n -> p t n", t=PACK))
             raw_of[j] = raw
 
-        def regroup(j):
-            grouped = grouped_pool.tile([P, SLAB_COLS, PACK], BF16, align_bytes=64)
-            if j < S:
-                dst = grouped[:].rearrange("p (g r m) t -> p g m t r", g=PASSES2, r=PACK)
-                src = raw_of[j][:].rearrange("p t (g m r) -> p g m t r", g=PASSES2, r=PACK)
-                cut = VECTOR_COLS // PASSES2 // PACK
+        def regroup(u):
+            j, c0, width = units[u]
+            raw = raw_of[j][:, :, c0 : c0 + width]
+            grouped = grouped_pool.tile([P, width, PACK], BF16, align_bytes=64, tag="grouped")
+            share = VECTOR_SHARE * width // SLAB_COLS
+            if slabs[j][0] == "W1":
+                halves = width // K_PASS
+                dst = grouped[:].rearrange("p (g r m) t -> p g m t r", g=halves, r=PACK)
+                src = raw.rearrange("p t (g m r) -> p g m t r", g=halves, r=PACK)
+                cut = share // halves // PACK
                 nc.vector.tensor_copy(out=dst[:, :, :cut], in_=src[:, :, :cut])
                 nc.scalar.copy(out=dst[:, :, cut:], in_=src[:, :, cut:])
             else:
                 dst = grouped[:].rearrange("p (c i) t -> p c t i", i=RUN)
-                src = raw_of[j][:].rearrange("p t (c i) -> p c t i", i=RUN)
-                cut = VECTOR_COLS // RUN
+                src = raw.rearrange("p t (c i) -> p c t i", i=RUN)
+                cut = share // RUN
                 nc.vector.tensor_copy(out=dst[:, :cut], in_=src[:, :cut])
                 nc.scalar.copy(out=dst[:, cut:], in_=src[:, cut:])
-            grouped_of[j] = grouped
+            grouped_of[u] = grouped
 
-        def quantise(j):
-            codes = codes_pool.tile([P, SLAB_COLS], U32, align_bytes=64)
-            scales = codes_pool.tile([P, SLAB_COLS], U8, align_bytes=64)
+        def quantise(u):
+            width = units[u][2]
+            codes = codes_pool.tile([P, width], U32, align_bytes=64, tag="codes")
+            scales = codes_pool.tile([P, width], U8, align_bytes=64, tag="scales")
             nc.vector.quantize_mx(
                 out=codes[:].bitcast(FP8X4),
                 scales=scales[:],
-                in_=grouped_of[j][:].rearrange("p c t -> p (c t)"),
+                in_=grouped_of[u][:].rearrange("p c t -> p (c t)"),
             )
-            codes_of[j] = (codes, scales)
+            codes_of[u] = (codes, scales)
 
-        def multiply(j):
-            codes, scales = codes_of[j]
-            if j < S:
-                h_acc_of[j] = []
-                for g in range(PASSES2):
-                    h_acc = h_psum.tile([P, PACK, B], F32)
+        def multiply(u):
+            j, c0, width = units[u]
+            matrix, s, where = slabs[j]
+            codes, scales = codes_of[u]
+            if matrix == "W1":
+                for half in range(width // K_PASS):
+                    h_acc = h_psum.tile([P, PACK, B], F32, tag="h")
                     for t in range(PACK):
-                        feats = slice((g * PACK + t) * P, (g * PACK + t + 1) * P)
+                        feats = slice((half * PACK + t) * P, (half * PACK + t + 1) * P)
                         nc.tensor.matmul_mx(
                             out=h_acc[:, t, :],
                             lhsT=codes[:, feats].bitcast(FP8X4),
                             lhsT_scale=scales[:, feats],
-                            rhs=x_codes[:, j * B : (j + 1) * B].bitcast(FP8X4),
-                            rhs_scale=x_scales[:, j * B : (j + 1) * B],
+                            rhs=x_codes[:, s * B : (s + 1) * B].bitcast(FP8X4),
+                            rhs_scale=x_scales[:, s * B : (s + 1) * B],
                             start=True,
                             stop=True,
                         )
-                    h_acc_of[j].append(h_acc)
+                    h_acc_of[(s, half if where is None else where)] = h_acc
             else:
-                s, g, w = w2_place(j)
+                g, w = where
                 h_codes, h_scales = h_codes_of[s]
-                for i in range(PASSES_PER_SLAB):
-                    n = w * PASSES_PER_SLAB + i
+                for i in range(width // N_PASS):
+                    n = (w * SLAB_COLS + c0) // N_PASS + i
                     if g == 0:
-                        bank = acc_psum.tile([P, N_PASS], F32)
+                        bank = acc_psum.tile([P, N_PASS], F32, tag="acc")
                         acc_of[(s, n)] = bank
                     nc.tensor.matmul_mx(
                         out=acc_of[(s, n)][:],
@@ -133,45 +149,54 @@ def tile_simplefusionmodule_pa_kernel(tc, x1, x2, W1, b1, W2, b2, out):
                         stop=(g == PASSES2 - 1),
                     )
 
-        def drain_h(s):
-            h_grouped = style_pool.tile([P, PASSES2, B, PACK], BF16, align_bytes=64)
-            h_codes = h_pool.tile([P, PASSES2 * B], U32, align_bytes=64)
-            h_scales = h_pool.tile([P, PASSES2 * B], U8, align_bytes=64)
-            for g in range(PASSES2):
-                b1_row = s * PASSES2 + g
+        def drain_h(s, halves):
+            if s not in h_grouped_of:
+                h_grouped = style_pool.tile([P, PASSES2, B, PACK], BF16, align_bytes=64)
+                h_grouped_of[s] = h_grouped
+            for g in halves:
                 nc.vector.tensor_tensor(
-                    out=h_grouped[:, g],
-                    in0=h_acc_of[s][g][:].rearrange("p t b -> p b t"),
-                    in1=b1_cols[:, b1_row].unsqueeze(1).to_broadcast([P, B, PACK]),
+                    out=h_grouped_of[s][:, g],
+                    in0=h_acc_of[(s, g)][:].rearrange("p t b -> p b t"),
+                    in1=b1_cols[:, s * PASSES2 + g].unsqueeze(1).to_broadcast([P, B, PACK]),
                     op=ADD,
                 )
-            for g in range(PASSES2):
-                nc.vector.tensor_scalar_max(h_grouped[:, g], h_grouped[:, g], 0.0)
-            for g in range(PASSES2):
-                nc.vector.quantize_mx(
-                    out=h_codes[:, g * B : (g + 1) * B].bitcast(FP8X4),
-                    scales=h_scales[:, g * B : (g + 1) * B],
-                    in_=h_grouped[:, g].rearrange("p b t -> p (b t)"),
-                )
+
+        def relu_h(s):
+            h_grouped = h_grouped_of[s]
+            nc.vector.tensor_scalar_max(h_grouped[:], h_grouped[:], 0.0)
+
+        def quantise_h(s):
+            h_codes = h_pool.tile([P, PASSES2 * B], U32, align_bytes=64)
+            h_scales = h_pool.tile([P, PASSES2 * B], U8, align_bytes=64)
+            nc.vector.quantize_mx(
+                out=h_codes[:].bitcast(FP8X4),
+                scales=h_scales[:],
+                in_=h_grouped_of[s][:].rearrange("p g b t -> p (g b t)"),
+            )
             h_codes_of[s] = (h_codes, h_scales)
 
-        def drain_out(s, w):
-            for i in range(PASSES_PER_SLAB):
-                n = w * PASSES_PER_SLAB + i
-                cols = slice(n * N_PASS, (n + 1) * N_PASS)
-                result = out_pool.tile([P, N_PASS], F32)
-                nc.vector.tensor_tensor(
-                    out=result[:], in0=acc_of[(s, n)][:], in1=b2_of[s][:, cols], op=ADD
-                )
-                nc.sync.dma_start(out=out[:, s, cols], in_=result[:])
+        def drain_out(s, n):
+            cols = slice(n * N_PASS, (n + 1) * N_PASS)
+            result = out_pool.tile([P, N_PASS], F32)
+            nc.vector.tensor_tensor(
+                out=result[:], in0=acc_of[(s, n)][:], in1=b2_of[s][:, cols], op=ADD
+            )
+            nc.sync.dma_start(out=out[:, s, cols], in_=result[:])
 
-        def drain(j):
-            if j < S:
-                drain_h(j)
-            else:
-                s, g, w = w2_place(j)
-                if g == PASSES2 - 1:
-                    drain_out(s, w)
+        def drain(u):
+            j, c0, width = units[u]
+            matrix, s, where = slabs[j]
+            if matrix == "W1":
+                drain_h(s, range(PASSES2) if where is None else [where])
+            elif where[0] == PASSES2 - 1:
+                for i in range(width // N_PASS):
+                    drain_out(s, (where[1] * SLAB_COLS + c0) // N_PASS + i)
+
+        def closes_h(u):
+            if not 0 <= u < len(units):
+                return None
+            matrix, s, where = slabs[units[u][0]]
+            return s if matrix == "W1" and where in (None, PASSES2 - 1) else None
 
         def spread_b2(s):
             spread_of[s] = []
@@ -196,73 +221,92 @@ def tile_simplefusionmodule_pa_kernel(tc, x1, x2, W1, b1, W2, b2, out):
 
         B1_ROWS = S * PASSES2
         B2_ROWS = S * F2 // P
+        load(0)
+        load(1)
         b1_rows = const.tile([P, K_PASS], BF16)
         nc.vector.memset(b1_rows[:], 0.0)
-        nc.sync.dma_start(
+        nc.scalar.dma_start(
             out=b1_rows[0:B1_ROWS, :], in_=b1.rearrange("s (g k) -> (s g) k", k=K_PASS)
         )
         b2_rows = const.tile([P, P], BF16)
         nc.vector.memset(b2_rows[B2_ROWS:P, :], 0.0)
-        nc.sync.dma_start(
+        nc.scalar.dma_start(
             out=b2_rows[0:B2_ROWS, :], in_=b2.rearrange("s (c p) -> (s c) p", p=P)
         )
         x_both = const.tile([P, S, STREAMS * D], BF16)
         nc.sync.dma_start(out=x_both[:, :, 0:D], in_=x1)
         nc.sync.dma_start(out=x_both[:, :, D : STREAMS * D], in_=x2)
-        for j in range(RESIDENT):
+        AHEAD = RESIDENT + 2
+        for j in range(2, AHEAD):
             load(j)
 
-        ident_bf = const.tile([P, P], BF16)
-        make_identity(nc, ident_bf[:])
         ident_f32 = const.tile([P, P], F32)
         make_identity(nc, ident_f32[:])
-
-        bias_cols = prep_psum.tile([P, PACK + 1, P], BF16, tag="prep")
-        for t in range(PACK):
-            nc.tensor.transpose(bias_cols[:, t], b1_rows[:, t:K_PASS:PACK], ident_bf[:])
-        nc.tensor.transpose(bias_cols[:, PACK], b2_rows[:], ident_bf[:])
-        b1_cols = const.tile([P, B1_ROWS, PACK], F32)
-        nc.vector.tensor_copy(
-            out=b1_cols[:], in_=bias_cols[:, 0:PACK, 0:B1_ROWS].rearrange("p t r -> p r t")
-        )
-        b2_cols = const.tile([P, B2_ROWS], BF16)
-        nc.vector.tensor_copy(out=b2_cols[:], in_=bias_cols[:, PACK, 0:B2_ROWS])
+        ident_bf = const.tile([P, P], BF16)
+        make_identity(nc, ident_bf[:])
 
         x_words = x_both[:].bitcast(F32)
         x_grouped = const.tile([P, S, B, PAIR], F32, align_bytes=64)
+        x_codes = const.tile([P, S * B], U32, align_bytes=64)
+        x_scales = const.tile([P, S * B], U8, align_bytes=64)
         STYLES_PER_BANK = 2
-        for s0 in range(0, S, STYLES_PER_BANK):
+
+        def transpose_x(s0):
             x_t = prep_psum.tile([P, STYLES_PER_BANK, PAIR, B], F32, tag="prep")
             for i in range(STYLES_PER_BANK):
                 for u in range(PAIR):
                     nc.tensor.transpose(x_t[:, i, u, :], x_words[:, s0 + i, u::PAIR], ident_f32[:])
-            nc.vector.tensor_copy(
+            nc.scalar.copy(
                 out=x_grouped[:, s0 : s0 + STYLES_PER_BANK],
                 in_=x_t[:].rearrange("p s u b -> p s b u"),
             )
-        x_codes = const.tile([P, S * B], U32, align_bytes=64)
-        x_scales = const.tile([P, S * B], U8, align_bytes=64)
-        nc.vector.quantize_mx(
-            out=x_codes[:].bitcast(FP8X4),
-            scales=x_scales[:],
-            in_=x_grouped[:].bitcast(BF16).rearrange("p s b t -> p (s b t)"),
-        )
-        spread_b2(0)
 
-        for step in range(SLABS + 3):
-            if step < SLABS:
+        def quantise_x():
+            nc.vector.quantize_mx(
+                out=x_codes[:].bitcast(FP8X4),
+                scales=x_scales[:],
+                in_=x_grouped[:].bitcast(BF16).rearrange("p s b t -> p (s b t)"),
+            )
+
+        b1_cols = const.tile([P, B1_ROWS, PACK], F32)
+        b2_cols = const.tile([P, B2_ROWS], BF16)
+
+        def transpose_biases():
+            bias_cols = prep_psum.tile([P, PACK + 1, P], BF16, tag="prep")
+            for t in range(PACK):
+                nc.tensor.transpose(bias_cols[:, t], b1_rows[:, t:K_PASS:PACK], ident_bf[:])
+            nc.tensor.transpose(bias_cols[:, PACK], b2_rows[:], ident_bf[:])
+            nc.vector.tensor_copy(
+                out=b1_cols[:], in_=bias_cols[:, 0:PACK, 0:B1_ROWS].rearrange("p t r -> p r t")
+            )
+            nc.vector.tensor_copy(out=b2_cols[:], in_=bias_cols[:, PACK, 0:B2_ROWS])
+
+        for step in range(len(units) + 3):
+            if step < len(units):
                 regroup(step)
-                if step + RESIDENT < SLABS:
-                    load(step + RESIDENT)
-                if step >= S:
-                    s, g, w = w2_place(step)
-                    if (g, w) == (0, 0):
+                j, c0, width = units[step]
+                if step == 1:
+                    for s0 in range(0, S, STYLES_PER_BANK):
+                        transpose_x(s0)
+                if step == 2:
+                    quantise_x()
+                    transpose_biases()
+                    spread_b2(0)
+                if j >= 2 and j + RESIDENT < len(slabs):
+                    load(j + RESIDENT)
+                matrix, s, where = slabs[j]
+                if matrix == "W2" and c0 == 0:
+                    if where == (0, 0):
                         copy_b2(s)
-                    if (g, w) == (0, 1) and s + 1 < S:
+                    if where == (1, 0) and s + 1 < S:
                         spread_b2(s + 1)
-            if 0 <= step - 1 < SLABS:
-                quantise(step - 1)
+            if closes_h(step - 4) is not None:
+                quantise_h(closes_h(step - 4))
             if 0 <= step - 3:
                 drain(step - 3)
-            if 0 <= step - 2 < SLABS:
+            if 0 <= step - 1 < len(units):
+                quantise(step - 1)
+            if closes_h(step - 3) is not None:
+                relu_h(closes_h(step - 3))
+            if 0 <= step - 2 < len(units):
                 multiply(step - 2)

@@ -19,15 +19,11 @@ STREAMS = 2
 PAIR = 2
 PASSES2 = F1 // K_PASS
 N_PASS = 512
-SLAB_COLS = 1024
-PASSES_PER_SLAB = SLAB_COLS // N_PASS
-HALVES = F2 // SLAB_COLS
-SLABS_PER_W2 = PASSES2 * HALVES
-SLABS = S + S * SLABS_PER_W2
-RESIDENT = 14
+UNIT_COLS = 1024
+RESIDENT = 5
 RUN = 4
 
-VECTOR_SHARE = 400
+VECTOR_SHARE = 432
 
 FLOPS = 2 * B * S * (STREAMS * D * F1 + F1 * F2)
 
@@ -37,24 +33,29 @@ def tile_simplefusionmodule_pa_kernel(tc, x1, x2, W1, b1, W2, b2, out):
     with ExitStack() as ctx:
         ctx.enter_context(tc.manual_schedule())
         const = ctx.enter_context(tc.tile_pool(name="const", bufs=1))
-        raw_pool = ctx.enter_context(tc.tile_pool(name="raw_pool", bufs=RESIDENT))
+        w1_pool = ctx.enter_context(tc.tile_pool(name="w1_pool", bufs=S - 1))
+        w2_pool = ctx.enter_context(tc.tile_pool(name="w2_pool", bufs=RESIDENT))
         grouped_pool = ctx.enter_context(tc.tile_pool(name="grouped_pool", bufs=4))
         codes_pool = ctx.enter_context(tc.tile_pool(name="codes_pool", bufs=4))
         style_pool = ctx.enter_context(tc.tile_pool(name="style_pool", bufs=2))
         h_pool = ctx.enter_context(tc.tile_pool(name="h_pool", bufs=S))
-        out_pool = ctx.enter_context(tc.tile_pool(name="out_pool", bufs=10))
+        out_pool = ctx.enter_context(tc.tile_pool(name="out_pool", bufs=6))
         prep_psum = ctx.enter_context(tc.psum_pool(name="prep_psum", bufs=2))
         h_psum = ctx.enter_context(tc.psum_pool(name="h_psum", bufs=PASSES2))
         acc_psum = ctx.enter_context(tc.psum_pool(name="acc_psum", bufs=F2 // N_PASS))
 
-        W1_SLABS = [("W1", 0, 0), ("W1", 0, 1)] + [("W1", s, None) for s in range(1, S)]
-        W2_SLABS = [("W2", s, (g, w)) for s in range(S) for w in range(HALVES) for g in range(PASSES2)]
-        slabs = W1_SLABS + W2_SLABS
-        units = [(j, 0, SLAB_COLS) for j in range(len(slabs))]
-        units[0] = (0, 0, K_PASS)
-        units[1] = (1, 0, K_PASS)
-        j_last = len(slabs) - 1
-        units[-2:] = [(j, c, N_PASS) for c in (0, N_PASS) for j in (j_last - 1, j_last)]
+        slabs = [("W1", 0, 0), ("W1", 0, 1)] + [("W1", s, None) for s in range(1, S)]
+        W1_SLABS = len(slabs)
+        slabs += [("W2", s, g) for s in range(S) for g in range(PASSES2)]
+        units = [(0, 0, K_PASS), (1, 0, K_PASS)] + [(j, 0, F1) for j in range(2, W1_SLABS)]
+        for s in range(S):
+            widths = [UNIT_COLS] * (F2 // UNIT_COLS)
+            if s == S - 1:
+                widths[-1:] = [N_PASS] * (UNIT_COLS // N_PASS)
+            c0 = 0
+            for width in widths:
+                units += [(W1_SLABS + s * PASSES2 + g, c0, width) for g in range(PASSES2)]
+                c0 += width
 
         raw_of = {}
         grouped_of = {}
@@ -69,15 +70,14 @@ def tile_simplefusionmodule_pa_kernel(tc, x1, x2, W1, b1, W2, b2, out):
         def load(j):
             matrix, s, where = slabs[j]
             if matrix == "W1" and where is None:
-                raw = raw_pool.tile([P, PACK, SLAB_COLS], BF16, tag="raw")
+                raw = w1_pool.tile([P, PACK, F1], BF16, tag="w1")
                 part = W1[s]
             elif matrix == "W1":
                 raw = const.tile([P, PACK, K_PASS], BF16, tag="first%d" % where)
                 part = W1[s, :, where * K_PASS : (where + 1) * K_PASS]
             else:
-                g, w = where
-                raw = raw_pool.tile([P, PACK, SLAB_COLS], BF16, tag="raw")
-                part = W2[s, g * K_PASS : (g + 1) * K_PASS, w * SLAB_COLS : (w + 1) * SLAB_COLS]
+                raw = w2_pool.tile([P, PACK, F2], BF16, tag="w2")
+                part = W2[s, where * K_PASS : (where + 1) * K_PASS]
             nc.sync.dma_start(out=raw[:], in_=part.rearrange("(p t) n -> p t n", t=PACK))
             raw_of[j] = raw
 
@@ -85,7 +85,7 @@ def tile_simplefusionmodule_pa_kernel(tc, x1, x2, W1, b1, W2, b2, out):
             j, c0, width = units[u]
             raw = raw_of[j][:, :, c0 : c0 + width]
             grouped = grouped_pool.tile([P, width, PACK], BF16, align_bytes=64, tag="grouped")
-            share = VECTOR_SHARE * width // SLAB_COLS
+            share = VECTOR_SHARE * width // UNIT_COLS
             if slabs[j][0] == "W1":
                 halves = width // K_PASS
                 dst = grouped[:].rearrange("p (g r m) t -> p g m t r", g=halves, r=PACK)
@@ -132,10 +132,10 @@ def tile_simplefusionmodule_pa_kernel(tc, x1, x2, W1, b1, W2, b2, out):
                         )
                     h_acc_of[(s, half if where is None else where)] = h_acc
             else:
-                g, w = where
+                g = where
                 h_codes, h_scales = h_codes_of[s]
                 for i in range(width // N_PASS):
-                    n = (w * SLAB_COLS + c0) // N_PASS + i
+                    n = c0 // N_PASS + i
                     if g == 0:
                         bank = acc_psum.tile([P, N_PASS], F32, tag="acc")
                         acc_of[(s, n)] = bank
@@ -175,22 +175,24 @@ def tile_simplefusionmodule_pa_kernel(tc, x1, x2, W1, b1, W2, b2, out):
             )
             h_codes_of[s] = (h_codes, h_scales)
 
-        def drain_out(s, n):
-            cols = slice(n * N_PASS, (n + 1) * N_PASS)
-            result = out_pool.tile([P, N_PASS], F32)
-            nc.vector.tensor_tensor(
-                out=result[:], in0=acc_of[(s, n)][:], in1=b2_of[s][:, cols], op=ADD
-            )
-            nc.sync.dma_start(out=out[:, s, cols], in_=result[:])
+        def drain_out(s, c0, width):
+            result = out_pool.tile([P, width], F32, tag="result")
+            for c in range(0, width, N_PASS):
+                nc.vector.tensor_tensor(
+                    out=result[:, c : c + N_PASS],
+                    in0=acc_of[(s, (c0 + c) // N_PASS)][:],
+                    in1=b2_of[s][:, c0 + c : c0 + c + N_PASS],
+                    op=ADD,
+                )
+            nc.sync.dma_start(out=out[:, s, c0 : c0 + width], in_=result[:])
 
         def drain(u):
             j, c0, width = units[u]
             matrix, s, where = slabs[j]
             if matrix == "W1":
                 drain_h(s, range(PASSES2) if where is None else [where])
-            elif where[0] == PASSES2 - 1:
-                for i in range(width // N_PASS):
-                    drain_out(s, (where[1] * SLAB_COLS + c0) // N_PASS + i)
+            elif where == PASSES2 - 1:
+                drain_out(s, c0, width)
 
         def closes_h(u):
             if not 0 <= u < len(units):
@@ -200,10 +202,10 @@ def tile_simplefusionmodule_pa_kernel(tc, x1, x2, W1, b1, W2, b2, out):
 
         def spread_b2(s):
             spread_of[s] = []
-            for w in range(HALVES):
-                spread = prep_psum.tile([P, SLAB_COLS], BF16, tag="prep")
-                for c in range(SLAB_COLS // P):
-                    col = (s * F2 + w * SLAB_COLS) // P + c
+            for w in range(F2 // UNIT_COLS):
+                spread = prep_psum.tile([P, UNIT_COLS], BF16, tag="prep")
+                for c in range(UNIT_COLS // P):
+                    col = (s * F2 + w * UNIT_COLS) // P + c
                     nc.tensor.transpose(
                         spread[:, c * P : (c + 1) * P],
                         b2_cols[:, col : col + 1].to_broadcast([P, P]),
@@ -213,9 +215,9 @@ def tile_simplefusionmodule_pa_kernel(tc, x1, x2, W1, b1, W2, b2, out):
 
         def copy_b2(s):
             b2_all = style_pool.tile([P, F2], BF16)
-            for w in range(HALVES):
+            for w in range(F2 // UNIT_COLS):
                 nc.scalar.copy(
-                    out=b2_all[:, w * SLAB_COLS : (w + 1) * SLAB_COLS], in_=spread_of[s][w][:]
+                    out=b2_all[:, w * UNIT_COLS : (w + 1) * UNIT_COLS], in_=spread_of[s][w][:]
                 )
             b2_of[s] = b2_all
 
@@ -236,8 +238,7 @@ def tile_simplefusionmodule_pa_kernel(tc, x1, x2, W1, b1, W2, b2, out):
         x_both = const.tile([P, S, STREAMS * D], BF16)
         nc.sync.dma_start(out=x_both[:, :, 0:D], in_=x1)
         nc.sync.dma_start(out=x_both[:, :, D : STREAMS * D], in_=x2)
-        AHEAD = RESIDENT + 2
-        for j in range(2, AHEAD):
+        for j in range(2, W1_SLABS + RESIDENT):
             load(j)
 
         ident_f32 = const.tile([P, P], F32)
@@ -292,13 +293,13 @@ def tile_simplefusionmodule_pa_kernel(tc, x1, x2, W1, b1, W2, b2, out):
                     quantise_x()
                     transpose_biases()
                     spread_b2(0)
-                if j >= 2 and j + RESIDENT < len(slabs):
-                    load(j + RESIDENT)
                 matrix, s, where = slabs[j]
-                if matrix == "W2" and c0 == 0:
-                    if where == (0, 0):
+                if matrix == "W2":
+                    if c0 + width == F2 and j + RESIDENT < len(slabs):
+                        load(j + RESIDENT)
+                    if (where, c0) == (0, 0):
                         copy_b2(s)
-                    if where == (1, 0) and s + 1 < S:
+                    if (where, c0) == (1, 0) and s + 1 < S:
                         spread_b2(s + 1)
             if closes_h(step - 4) is not None:
                 quantise_h(closes_h(step - 4))

@@ -9,6 +9,7 @@ U32 = mybir.dt.uint32
 U8 = mybir.dt.uint8
 FP8X4 = mybir.dt.float8_e4m3fn_x4
 ADD = mybir.AluOpType.add
+MULT = mybir.AluOpType.mult
 
 P = 128
 PACK = 4
@@ -23,7 +24,11 @@ UNIT_COLS = 1024
 RESIDENT = 5
 RUN = 4
 
-VECTOR_SHARE = 432
+VECTOR_SHARE = 352
+
+GPSIMD_COLS = 192
+
+PE_COLS = 256
 
 FLOPS = 2 * B * S * (STREAMS * D * F1 + F1 * F2)
 
@@ -58,6 +63,7 @@ def tile_simplefusionmodule_pa_kernel(tc, x1, x2, W1, b1, W2, b2, out):
                 c0 += width
 
         raw_of = {}
+        moved_of = {}
         grouped_of = {}
         codes_of = {}
         h_acc_of = {}
@@ -97,9 +103,52 @@ def tile_simplefusionmodule_pa_kernel(tc, x1, x2, W1, b1, W2, b2, out):
                 dst = grouped[:].rearrange("p (c i) t -> p c t i", i=RUN)
                 src = raw.rearrange("p t (c i) -> p c t i", i=RUN)
                 cut = share // RUN
+                scalar_cut = cut
+                if empties_two_banks(u - 3):
+                    scalar_cut = cut + GPSIMD_COLS // RUN
+                end = (width - PE_COLS if u in moved_of else width) // RUN
                 nc.vector.tensor_copy(out=dst[:, :cut], in_=src[:, :cut])
-                nc.scalar.copy(out=dst[:, cut:], in_=src[:, cut:])
+                nc.scalar.copy(out=dst[:, scalar_cut:end], in_=src[:, scalar_cut:end])
+                if scalar_cut > cut:
+                    nc.gpsimd.tensor_scalar(
+                        out=dst[:, cut - 1 : scalar_cut],
+                        in0=src[:, cut - 1 : scalar_cut],
+                        scalar1=1.0,
+                        scalar2=0.0,
+                        op0=MULT,
+                        op1=ADD,
+                    )
+                if u in moved_of:
+                    nc.scalar.copy(out=grouped[:, width - PE_COLS :], in_=moved_of[u][:])
             grouped_of[u] = grouped
+
+        def empties_two_banks(u):
+            j, c0, width = units[u]
+            matrix, s, where = slabs[j]
+            if matrix == "W1":
+                return width > K_PASS
+            return where == PASSES2 - 1 and width > N_PASS
+
+        def by_tensor_engine(u):
+            if u >= len(units):
+                return False
+            j, c0, width = units[u]
+            return j > W1_SLABS + 1 and slabs[j][2] == PASSES2 - 1 and width == UNIT_COLS
+
+        def move(u):
+            j, c0, width = units[u]
+            moved = h_psum.tile([P, PE_COLS, PACK], BF16, tag="h")
+            step = N_PASS // PACK
+            for c in range(0, PE_COLS, step):
+                first = c0 + width - PE_COLS + c
+                nc.tensor.matmul(
+                    out=moved[:, c : c + step, :].rearrange("p c t -> p (c t)"),
+                    lhsT=ident_bf[:],
+                    rhs=raw_of[j][:, :, first : first + step].rearrange("p t c -> p c t"),
+                    start=True,
+                    stop=True,
+                )
+            moved_of[u] = moved
 
         def quantise(u):
             width = units[u][2]
@@ -309,5 +358,7 @@ def tile_simplefusionmodule_pa_kernel(tc, x1, x2, W1, b1, W2, b2, out):
                 quantise(step - 1)
             if closes_h(step - 3) is not None:
                 relu_h(closes_h(step - 3))
+            if by_tensor_engine(step + 1):
+                move(step + 1)
             if 0 <= step - 2 < len(units):
                 multiply(step - 2)

@@ -24,7 +24,7 @@ UNIT_COLS = 1024
 RESIDENT = 5
 RUN = 4
 
-VECTOR_SHARE = 352
+VECTOR_SHARE = 304
 
 GPSIMD_COLS = 192
 

from contextlib import ExitStack

import concourse.mybir as mybir
from concourse.masks import make_identity

BF16 = mybir.dt.bfloat16
F32 = mybir.dt.float32
U32 = mybir.dt.uint32
U8 = mybir.dt.uint8
FP8X4 = mybir.dt.float8_e4m3fn_x4
ADD = mybir.AluOpType.add
MULT = mybir.AluOpType.mult

P = 128
PACK = 4
K_PASS = P * PACK

B, S, D, F1, F2 = 128, 4, 256, 1024, 2048
STREAMS = 2
PAIR = 2
PASSES2 = F1 // K_PASS
N_PASS = 512
UNIT_COLS = 1024
RESIDENT = 5
RUN = 4

VECTOR_SHARE = 304

GPSIMD_COLS = 192

PE_COLS = 256

FLOPS = 2 * B * S * (STREAMS * D * F1 + F1 * F2)


def tile_simplefusionmodule_pa_kernel(tc, x1, x2, W1, b1, W2, b2, out):
    nc = tc.nc
    with ExitStack() as ctx:
        ctx.enter_context(tc.manual_schedule())
        const = ctx.enter_context(tc.tile_pool(name="const", bufs=1))
        w1_pool = ctx.enter_context(tc.tile_pool(name="w1_pool", bufs=S - 1))
        w2_pool = ctx.enter_context(tc.tile_pool(name="w2_pool", bufs=RESIDENT))
        grouped_pool = ctx.enter_context(tc.tile_pool(name="grouped_pool", bufs=4))
        codes_pool = ctx.enter_context(tc.tile_pool(name="codes_pool", bufs=4))
        style_pool = ctx.enter_context(tc.tile_pool(name="style_pool", bufs=2))
        h_pool = ctx.enter_context(tc.tile_pool(name="h_pool", bufs=S))
        out_pool = ctx.enter_context(tc.tile_pool(name="out_pool", bufs=6))
        prep_psum = ctx.enter_context(tc.psum_pool(name="prep_psum", bufs=2))
        h_psum = ctx.enter_context(tc.psum_pool(name="h_psum", bufs=PASSES2))
        acc_psum = ctx.enter_context(tc.psum_pool(name="acc_psum", bufs=F2 // N_PASS))

        slabs = [("W1", 0, 0), ("W1", 0, 1)] + [("W1", s, None) for s in range(1, S)]
        W1_SLABS = len(slabs)
        slabs += [("W2", s, g) for s in range(S) for g in range(PASSES2)]
        units = [(0, 0, K_PASS), (1, 0, K_PASS)] + [(j, 0, F1) for j in range(2, W1_SLABS)]
        for s in range(S):
            widths = [UNIT_COLS] * (F2 // UNIT_COLS)
            if s == S - 1:
                widths[-1:] = [N_PASS] * (UNIT_COLS // N_PASS)
            c0 = 0
            for width in widths:
                units += [(W1_SLABS + s * PASSES2 + g, c0, width) for g in range(PASSES2)]
                c0 += width

        raw_of = {}
        moved_of = {}
        grouped_of = {}
        codes_of = {}
        h_acc_of = {}
        h_grouped_of = {}
        h_codes_of = {}
        acc_of = {}
        spread_of = {}
        b2_of = {}

        def load(j):
            matrix, s, where = slabs[j]
            if matrix == "W1" and where is None:
                raw = w1_pool.tile([P, PACK, F1], BF16, tag="w1")
                part = W1[s]
            elif matrix == "W1":
                raw = const.tile([P, PACK, K_PASS], BF16, tag="first%d" % where)
                part = W1[s, :, where * K_PASS : (where + 1) * K_PASS]
            else:
                raw = w2_pool.tile([P, PACK, F2], BF16, tag="w2")
                part = W2[s, where * K_PASS : (where + 1) * K_PASS]
            nc.sync.dma_start(out=raw[:], in_=part.rearrange("(p t) n -> p t n", t=PACK))
            raw_of[j] = raw

        def regroup(u):
            j, c0, width = units[u]
            raw = raw_of[j][:, :, c0 : c0 + width]
            grouped = grouped_pool.tile([P, width, PACK], BF16, align_bytes=64, tag="grouped")
            share = VECTOR_SHARE * width // UNIT_COLS
            if slabs[j][0] == "W1":
                halves = width // K_PASS
                dst = grouped[:].rearrange("p (g r m) t -> p g m t r", g=halves, r=PACK)
                src = raw.rearrange("p t (g m r) -> p g m t r", g=halves, r=PACK)
                cut = share // halves // PACK
                nc.vector.tensor_copy(out=dst[:, :, :cut], in_=src[:, :, :cut])
                nc.scalar.copy(out=dst[:, :, cut:], in_=src[:, :, cut:])
            else:
                dst = grouped[:].rearrange("p (c i) t -> p c t i", i=RUN)
                src = raw.rearrange("p t (c i) -> p c t i", i=RUN)
                cut = share // RUN
                scalar_cut = cut
                if empties_two_banks(u - 3):
                    scalar_cut = cut + GPSIMD_COLS // RUN
                end = (width - PE_COLS if u in moved_of else width) // RUN
                nc.vector.tensor_copy(out=dst[:, :cut], in_=src[:, :cut])
                nc.scalar.copy(out=dst[:, scalar_cut:end], in_=src[:, scalar_cut:end])
                if scalar_cut > cut:
                    nc.gpsimd.tensor_scalar(
                        out=dst[:, cut - 1 : scalar_cut],
                        in0=src[:, cut - 1 : scalar_cut],
                        scalar1=1.0,
                        scalar2=0.0,
                        op0=MULT,
                        op1=ADD,
                    )
                if u in moved_of:
                    nc.scalar.copy(out=grouped[:, width - PE_COLS :], in_=moved_of[u][:])
            grouped_of[u] = grouped

        def empties_two_banks(u):
            j, c0, width = units[u]
            matrix, s, where = slabs[j]
            if matrix == "W1":
                return width > K_PASS
            return where == PASSES2 - 1 and width > N_PASS

        def by_tensor_engine(u):
            if u >= len(units):
                return False
            j, c0, width = units[u]
            return j > W1_SLABS + 1 and slabs[j][2] == PASSES2 - 1 and width == UNIT_COLS

        def move(u):
            j, c0, width = units[u]
            moved = h_psum.tile([P, PE_COLS, PACK], BF16, tag="h")
            step = N_PASS // PACK
            for c in range(0, PE_COLS, step):
                first = c0 + width - PE_COLS + c
                nc.tensor.matmul(
                    out=moved[:, c : c + step, :].rearrange("p c t -> p (c t)"),
                    lhsT=ident_bf[:],
                    rhs=raw_of[j][:, :, first : first + step].rearrange("p t c -> p c t"),
                    start=True,
                    stop=True,
                )
            moved_of[u] = moved

        def quantise(u):
            width = units[u][2]
            codes = codes_pool.tile([P, width], U32, align_bytes=64, tag="codes")
            scales = codes_pool.tile([P, width], U8, align_bytes=64, tag="scales")
            nc.vector.quantize_mx(
                out=codes[:].bitcast(FP8X4),
                scales=scales[:],
                in_=grouped_of[u][:].rearrange("p c t -> p (c t)"),
            )
            codes_of[u] = (codes, scales)

        def multiply(u):
            j, c0, width = units[u]
            matrix, s, where = slabs[j]
            codes, scales = codes_of[u]
            if matrix == "W1":
                for half in range(width // K_PASS):
                    h_acc = h_psum.tile([P, PACK, B], F32, tag="h")
                    for t in range(PACK):
                        feats = slice((half * PACK + t) * P, (half * PACK + t + 1) * P)
                        nc.tensor.matmul_mx(
                            out=h_acc[:, t, :],
                            lhsT=codes[:, feats].bitcast(FP8X4),
                            lhsT_scale=scales[:, feats],
                            rhs=x_codes[:, s * B : (s + 1) * B].bitcast(FP8X4),
                            rhs_scale=x_scales[:, s * B : (s + 1) * B],
                            start=True,
                            stop=True,
                        )
                    h_acc_of[(s, half if where is None else where)] = h_acc
            else:
                g = where
                h_codes, h_scales = h_codes_of[s]
                for i in range(width // N_PASS):
                    n = c0 // N_PASS + i
                    if g == 0:
                        bank = acc_psum.tile([P, N_PASS], F32, tag="acc")
                        acc_of[(s, n)] = bank
                    nc.tensor.matmul_mx(
                        out=acc_of[(s, n)][:],
                        lhsT=h_codes[:, g * B : (g + 1) * B].bitcast(FP8X4),
                        lhsT_scale=h_scales[:, g * B : (g + 1) * B],
                        rhs=codes[:, i * N_PASS : (i + 1) * N_PASS].bitcast(FP8X4),
                        rhs_scale=scales[:, i * N_PASS : (i + 1) * N_PASS],
                        start=(g == 0),
                        stop=(g == PASSES2 - 1),
                    )

        def drain_h(s, halves):
            if s not in h_grouped_of:
                h_grouped = style_pool.tile([P, PASSES2, B, PACK], BF16, align_bytes=64)
                h_grouped_of[s] = h_grouped
            for g in halves:
                nc.vector.tensor_tensor(
                    out=h_grouped_of[s][:, g],
                    in0=h_acc_of[(s, g)][:].rearrange("p t b -> p b t"),
                    in1=b1_cols[:, s * PASSES2 + g].unsqueeze(1).to_broadcast([P, B, PACK]),
                    op=ADD,
                )

        def relu_h(s):
            h_grouped = h_grouped_of[s]
            nc.vector.tensor_scalar_max(h_grouped[:], h_grouped[:], 0.0)

        def quantise_h(s):
            h_codes = h_pool.tile([P, PASSES2 * B], U32, align_bytes=64)
            h_scales = h_pool.tile([P, PASSES2 * B], U8, align_bytes=64)
            nc.vector.quantize_mx(
                out=h_codes[:].bitcast(FP8X4),
                scales=h_scales[:],
                in_=h_grouped_of[s][:].rearrange("p g b t -> p (g b t)"),
            )
            h_codes_of[s] = (h_codes, h_scales)

        def drain_out(s, c0, width):
            result = out_pool.tile([P, width], F32, tag="result")
            for c in range(0, width, N_PASS):
                nc.vector.tensor_tensor(
                    out=result[:, c : c + N_PASS],
                    in0=acc_of[(s, (c0 + c) // N_PASS)][:],
                    in1=b2_of[s][:, c0 + c : c0 + c + N_PASS],
                    op=ADD,
                )
            nc.sync.dma_start(out=out[:, s, c0 : c0 + width], in_=result[:])

        def drain(u):
            j, c0, width = units[u]
            matrix, s, where = slabs[j]
            if matrix == "W1":
                drain_h(s, range(PASSES2) if where is None else [where])
            elif where == PASSES2 - 1:
                drain_out(s, c0, width)

        def closes_h(u):
            if not 0 <= u < len(units):
                return None
            matrix, s, where = slabs[units[u][0]]
            return s if matrix == "W1" and where in (None, PASSES2 - 1) else None

        def spread_b2(s):
            spread_of[s] = []
            for w in range(F2 // UNIT_COLS):
                spread = prep_psum.tile([P, UNIT_COLS], BF16, tag="prep")
                for c in range(UNIT_COLS // P):
                    col = (s * F2 + w * UNIT_COLS) // P + c
                    nc.tensor.transpose(
                        spread[:, c * P : (c + 1) * P],
                        b2_cols[:, col : col + 1].to_broadcast([P, P]),
                        ident_bf[:],
                    )
                spread_of[s].append(spread)

        def copy_b2(s):
            b2_all = style_pool.tile([P, F2], BF16)
            for w in range(F2 // UNIT_COLS):
                nc.scalar.copy(
                    out=b2_all[:, w * UNIT_COLS : (w + 1) * UNIT_COLS], in_=spread_of[s][w][:]
                )
            b2_of[s] = b2_all

        B1_ROWS = S * PASSES2
        B2_ROWS = S * F2 // P
        load(0)
        load(1)
        b1_rows = const.tile([P, K_PASS], BF16)
        nc.vector.memset(b1_rows[:], 0.0)
        nc.scalar.dma_start(
            out=b1_rows[0:B1_ROWS, :], in_=b1.rearrange("s (g k) -> (s g) k", k=K_PASS)
        )
        b2_rows = const.tile([P, P], BF16)
        nc.vector.memset(b2_rows[B2_ROWS:P, :], 0.0)
        nc.scalar.dma_start(
            out=b2_rows[0:B2_ROWS, :], in_=b2.rearrange("s (c p) -> (s c) p", p=P)
        )
        x_both = const.tile([P, S, STREAMS * D], BF16)
        nc.sync.dma_start(out=x_both[:, :, 0:D], in_=x1)
        nc.sync.dma_start(out=x_both[:, :, D : STREAMS * D], in_=x2)
        for j in range(2, W1_SLABS + RESIDENT):
            load(j)

        ident_f32 = const.tile([P, P], F32)
        make_identity(nc, ident_f32[:])
        ident_bf = const.tile([P, P], BF16)
        make_identity(nc, ident_bf[:])

        x_words = x_both[:].bitcast(F32)
        x_grouped = const.tile([P, S, B, PAIR], F32, align_bytes=64)
        x_codes = const.tile([P, S * B], U32, align_bytes=64)
        x_scales = const.tile([P, S * B], U8, align_bytes=64)
        STYLES_PER_BANK = 2

        def transpose_x(s0):
            x_t = prep_psum.tile([P, STYLES_PER_BANK, PAIR, B], F32, tag="prep")
            for i in range(STYLES_PER_BANK):
                for u in range(PAIR):
                    nc.tensor.transpose(x_t[:, i, u, :], x_words[:, s0 + i, u::PAIR], ident_f32[:])
            nc.scalar.copy(
                out=x_grouped[:, s0 : s0 + STYLES_PER_BANK],
                in_=x_t[:].rearrange("p s u b -> p s b u"),
            )

        def quantise_x():
            nc.vector.quantize_mx(
                out=x_codes[:].bitcast(FP8X4),
                scales=x_scales[:],
                in_=x_grouped[:].bitcast(BF16).rearrange("p s b t -> p (s b t)"),
            )

        b1_cols = const.tile([P, B1_ROWS, PACK], F32)
        b2_cols = const.tile([P, B2_ROWS], BF16)

        def transpose_biases():
            bias_cols = prep_psum.tile([P, PACK + 1, P], BF16, tag="prep")
            for t in range(PACK):
                nc.tensor.transpose(bias_cols[:, t], b1_rows[:, t:K_PASS:PACK], ident_bf[:])
            nc.tensor.transpose(bias_cols[:, PACK], b2_rows[:], ident_bf[:])
            nc.vector.tensor_copy(
                out=b1_cols[:], in_=bias_cols[:, 0:PACK, 0:B1_ROWS].rearrange("p t r -> p r t")
            )
            nc.vector.tensor_copy(out=b2_cols[:], in_=bias_cols[:, PACK, 0:B2_ROWS])

        for step in range(len(units) + 3):
            if step < len(units):
                regroup(step)
                j, c0, width = units[step]
                if step == 1:
                    for s0 in range(0, S, STYLES_PER_BANK):
                        transpose_x(s0)
                if step == 2:
                    quantise_x()
                    transpose_biases()
                    spread_b2(0)
                matrix, s, where = slabs[j]
                if matrix == "W2":
                    if c0 + width == F2 and j + RESIDENT < len(slabs):
                        load(j + RESIDENT)
                    if (where, c0) == (0, 0):
                        copy_b2(s)
                    if (where, c0) == (1, 0) and s + 1 < S:
                        spread_b2(s + 1)
            if closes_h(step - 4) is not None:
                quantise_h(closes_h(step - 4))
            if 0 <= step - 3:
                drain(step - 3)
            if 0 <= step - 1 < len(units):
                quantise(step - 1)
            if closes_h(step - 3) is not None:
                relu_h(closes_h(step - 3))
            if by_tensor_engine(step + 1):
                move(step + 1)
            if 0 <= step - 2 < len(units):
                multiply(step - 2)
